import numpy as np
import ml_dtypes


def mxq(x, axis, fmt="e4m3"):
    dtype, down = {"e4m3": (ml_dtypes.float8_e4m3fn, 7), "e5m2": (ml_dtypes.float8_e5m2, 14)}[fmt]
    v = np.moveaxis(np.asarray(x, np.float32).astype(ml_dtypes.bfloat16).astype(np.float64), axis, -1)
    blocks = v.reshape(v.shape[:-1] + (-1, 32))
    amax = np.abs(blocks).max(-1, keepdims=True)
    byte = np.maximum(np.where(amax > 0, np.frexp(amax)[1] - 1 + 127, 0) - down, 1)
    scale = np.exp2(byte - 127.0)
    codes = (blocks / scale).astype(np.float32).astype(dtype).astype(np.float64)
    return np.moveaxis((codes * scale).reshape(v.shape), -1, axis)


WIDE = False


def mx_kscale(k):
    if not WIDE:
        return np.ones(k)
    levels = np.array([10, -10, 5, -5, 0])
    if k % 512:
        return np.exp2(np.random.permutation(np.resize(levels, k // 32))).repeat(32)
    a = np.empty((k // 512, 16))
    for p in range(k // 512):
        a[p, :8] = np.random.permutation(np.resize(levels, 8))
        for g in range(8):
            far = levels[np.abs(levels - a[p, g]) >= 10]
            a[p, g + 8] = far[np.random.randint(len(far))]
    return np.exp2(a.ravel()).repeat(32)


BF16 = ml_dtypes.bfloat16


def bf(x):
    return np.asarray(x, np.float32).astype(BF16)


def f64(x):
    return np.asarray(x).astype(np.float64)


B, T, C, HS, DW, DA, DV, DG = 4, 1024, 1024, 64, 512, 128, 128, 224
H = C // HS


def setup_inputs():
    s = mx_kscale(C)
    return {
        "x": bf(np.random.standard_normal((B, T, C)) * s),
        "x_k": bf(np.random.uniform(0.0, 1.0, C)),
        "Wk": bf(np.random.standard_normal((C, C)) / np.sqrt(C) / s[None, :]),
        "k_k": bf(0.71 + 0.1 * np.random.standard_normal(C)),
    }


def reference(x, x_k, Wk, k_k):
    x = f64(x)
    xprev = np.concatenate([np.zeros_like(x[:, :1]), x[:, :-1]], axis=1)
    xx = xprev - x
    xk = x + xx * f64(x_k)
    k = mxq(xk, 2, "e4m3") @ mxq(f64(Wk), 1, "e4m3").T
    kk4 = (k * f64(k_k)).reshape(B, T, H, HS)
    nrm = np.sqrt((kk4 ** 2).sum(-1, keepdims=True))
    kk = (kk4 / np.maximum(nrm, 1e-12)).reshape(B, T, C)
    return kk

@@ -1,0 +1,330 @@
+from contextlib import ExitStack
+
+import concourse.mybir as mybir
+from concourse.masks import make_identity
+
+FP8X4 = mybir.dt.float8_e4m3fn_x4
+BF16 = mybir.dt.bfloat16
+F32 = mybir.dt.float32
+U32 = mybir.dt.uint32
+U8 = mybir.dt.uint8
+ALU = mybir.AluOpType
+ACT = mybir.ActivationFunctionType
+
+P = 128
+B, T, C = 4, 1024, 1024
+HEAD = 64
+HEADS = C // HEAD
+PACK = 4
+PAIRED = 2
+K_PASS = P * PACK
+PASSES = C // K_PASS
+WORDS = K_PASS // PAIRED
+CHUNK = 512
+CHUNKS = B * T // CHUNK
+SEQ_CHUNKS = T // CHUNK
+CHUNK_TILES = CHUNK // P
+BANKS = PASSES * PAIRED
+STEPS = CHUNKS * BANKS
+W_QUARTER = 256
+W_QUARTERS = C // W_QUARTER
+N_TILE = 512
+N_TILES = C // N_TILE
+PAIR = 2
+PIECE_HEADS = 8
+RUN = 4
+NORM_FLOOR = 1e-12
+TINY = 1e-34
+
+SHIFT_LAG = 1
+BLEND_LAG = 2
+QUANT_LAG = 3
+MULTIPLY_LAG = 7
+K_K_LAG = 8
+SUMS_LAG = 9
+NORMALISE_LAG = 10
+TICKS = STEPS + NORMALISE_LAG + 1
+
+FLOPS = 2 * B * T * C * C
+
+
+def tile_full_tmix_params_pa_t_kernel(tc, x, x_k, Wk, k_k, out):
+    nc = tc.nc
+    x_view = x.rearrange("b (i p) c -> p b i c", p=P)
+    w_view = Wk.rearrange("(r p) c -> p r c", p=P)
+    out_view = out.rearrange("b (i p) c -> p b i c", p=P)
+
+    with ExitStack() as ctx:
+        ctx.enter_context(tc.manual_schedule())
+        keep = ctx.enter_context(tc.tile_pool(name="keep", bufs=1))
+        w_stage = ctx.enter_context(tc.tile_pool(name="w_stage", bufs=PASSES))
+        mix_stage = ctx.enter_context(tc.tile_pool(name="mix_stage", bufs=2))
+        quantised = ctx.enter_context(tc.tile_pool(name="quantised", bufs=3 * PASSES))
+        results = ctx.enter_context(tc.tile_pool(name="results", bufs=5))
+        norms = ctx.enter_context(tc.tile_pool(name="norms", bufs=4))
+        scratch = ctx.enter_context(tc.tile_pool(name="scratch", bufs=2))
+        flipped = ctx.enter_context(tc.psum_pool(name="flipped", bufs=4))
+        products = ctx.enter_context(tc.psum_pool(name="products", bufs=4))
+
+        x_k_rows = keep.tile([P, K_PASS], BF16)
+        nc.vector.memset(x_k_rows[:], 0.0)
+        x_sb = keep.tile([P, B, T // P, C], BF16)
+        w_sb = keep.tile([P, C // P, C], BF16)
+        k_k_sb = keep.tile([P, C], BF16)
+
+        def load_x(chunk, cols):
+            s, h = divmod(chunk, SEQ_CHUNKS)
+            tiles = slice(h * CHUNK_TILES, (h + 1) * CHUNK_TILES)
+            nc.sync.dma_start(out=x_sb[:, s, tiles, cols], in_=x_view[:, s, tiles, cols])
+
+        first, second = slice(0, K_PASS), slice(K_PASS, C)
+        nc.sync.dma_start(out=x_k_rows[0:PASSES, :], in_=x_k.rearrange("(g c) -> g c", g=PASSES))
+        load_x(0, first)
+        load_x(0, second)
+        nc.sync.dma_start(out=w_sb[:, :, first], in_=w_view[:, :, first])
+        nc.sync.dma_start(out=w_sb[:, :, second], in_=w_view[:, :, second])
+        load_x(1, slice(0, C))
+        nc.sync.dma_start(out=k_k_sb[:], in_=k_k.partition_broadcast(P))
+        for chunk in range(2, CHUNKS):
+            load_x(chunk, slice(0, C))
+
+        ident = keep.tile([P, P], F32)
+        make_identity(nc, ident[:])
+
+        one = keep.tile([P, 1], F32)
+        nc.vector.memset(one[:], 1.0)
+        nc.scalar.activation(out=one[:], in_=one[:], func=ACT.Abs_reciprocal_sqrt)
+
+        x_k_words = x_k_rows[:].bitcast(F32)
+        x_k_flipped = flipped.tile([P, PAIRED, 2 * P], F32, tag="bank")
+        for u in range(PAIRED):
+            nc.tensor.transpose(x_k_flipped[:, u, 0:P], x_k_words[:, u:WORDS:PAIRED], ident[:])
+        mix_prev = keep.tile([P, PASSES, PAIRED, PAIRED], F32)
+        mix_here = keep.tile([P, PASSES, PAIRED, PAIRED], F32)
+        nc.vector.tensor_copy(
+            out=mix_prev[:].rearrange("p g u e -> p u g e"),
+            in_=x_k_flipped[:]
+            .rearrange("p u n -> p (u n)")
+            .bitcast(BF16)
+            .rearrange("p (u n e) -> p u n e", u=PAIRED, e=PAIRED)[:, :, 0:PASSES, :],
+        )
+        nc.vector.tensor_scalar(
+            out=mix_here[:], in0=mix_prev[:], scalar1=-1.0, scalar2=1.0, op0=ALU.mult, op1=ALU.add
+        )
+
+        prev = keep.tile([P, PASSES, PAIRED, PAIRED, T + 8], F32)
+        nc.vector.memset(prev[:, :, :, :, 0:8].rearrange("p g u e t -> p (g u e) t"), 0.0)
+
+        w_codes = keep.tile([P, PASSES, C], U32, align_bytes=64)
+        w_scales = keep.tile([P, PASSES, C], U8, align_bytes=64)
+
+        w_banks, w_grouped = {}, {}
+        x_banks, planes, grouped, xk_mx = {}, {}, {}, {}
+        accs, scaled, square_sums, inverse = {}, {}, {}, {}
+
+        def flip_weights(b):
+            g, quarter = divmod(b, W_QUARTERS)
+            w_banks[b] = flipped.tile([P, PAIRED, 2 * P], F32, tag="bank", name="w_bank")
+            for u in range(PAIRED):
+                for r in range(W_QUARTER // P):
+                    words = w_sb[:, quarter * (W_QUARTER // P) + r, :].bitcast(F32)
+                    nc.tensor.transpose(
+                        w_banks[b][:, u, r * P : (r + 1) * P],
+                        words[:, g * WORDS + u : (g + 1) * WORDS : PAIRED],
+                        ident[:],
+                    )
+
+        def group_weights(b):
+            g, quarter = divmod(b, W_QUARTERS)
+            if quarter == 0:
+                w_grouped[g] = w_stage.tile([P, C, PACK], BF16, align_bytes=64, name="w_grouped")
+            rows = slice(quarter * W_QUARTER, (quarter + 1) * W_QUARTER)
+            nc.scalar.copy(
+                out=w_grouped[g][:, rows, :].rearrange("p o j -> p (o j)").bitcast(F32),
+                in_=w_banks[b][:].rearrange("p u o -> p o u"),
+            )
+
+        def quantise_weights(g):
+            nc.vector.quantize_mx(
+                out=w_codes[:, g, :].bitcast(FP8X4),
+                scales=w_scales[:, g, :],
+                in_=w_grouped[g][:].rearrange("p o j -> p (o j)"),
+            )
+
+        def place(m):
+            chunk, within = divmod(m, BANKS)
+            g, u = divmod(within, PAIRED)
+            s, h = divmod(chunk, SEQ_CHUNKS)
+            return chunk, g, u, s, h
+
+        def flip(m):
+            chunk, g, u, s, h = place(m)
+            x_banks[m] = flipped.tile([P, PAIRED, 2 * P], F32, tag="bank", name="x_bank")
+            bank = x_banks[m][:].rearrange("p u n -> p (u n)")
+            for i in range(CHUNK_TILES):
+                words = x_sb[:, s, h * CHUNK_TILES + i, :].bitcast(F32)
+                nc.tensor.transpose(
+                    bank[:, i * P : (i + 1) * P],
+                    words[:, g * WORDS + u : (g + 1) * WORDS : PAIRED],
+                    ident[:],
+                )
+
+        def bank_view(m):
+            return (
+                x_banks[m][:]
+                .rearrange("p u n -> p (u n)")
+                .bitcast(BF16)
+                .rearrange("p (t e) -> p e t", e=PAIRED)
+            )
+
+        def shift(m):
+            chunk, g, u, s, h = place(m)
+            for e in range(PAIRED):
+                nc.scalar.activation(
+                    out=prev[:, g, u, e, 1 + h * CHUNK : 1 + (h + 1) * CHUNK],
+                    in_=bank_view(m)[:, e, :],
+                    func=ACT.Copy,
+                    scale=mix_prev[:, g, u, e : e + 1],
+                )
+
+        def blend(m):
+            chunk, g, u, s, h = place(m)
+            q = m // PAIRED
+            if u == 0:
+                planes[q] = mix_stage.tile([P, PACK, CHUNK], BF16, name="planes")
+            for e in range(PAIRED):
+                nc.vector.scalar_tensor_tensor(
+                    out=planes[q][:, u * PAIRED + e, :],
+                    in0=bank_view(m)[:, e, :],
+                    scalar=mix_here[:, g, u, e : e + 1],
+                    in1=prev[:, g, u, e, h * CHUNK : (h + 1) * CHUNK],
+                    op0=ALU.mult,
+                    op1=ALU.add,
+                )
+
+        def regroup(q):
+            grouped[q] = mix_stage.tile([P, CHUNK, PACK], BF16, align_bytes=64, name="grouped")
+            nc.vector.tensor_copy(
+                out=grouped[q][:].rearrange("p (c i) j -> p c j i", i=RUN),
+                in_=planes[q][:].rearrange("p j (c i) -> p c j i", i=RUN),
+            )
+
+        def quantise(q):
+            codes = quantised.tile([P, CHUNK], U32, align_bytes=64)
+            scales = quantised.tile([P, CHUNK], U8, align_bytes=64)
+            nc.vector.quantize_mx(
+                out=codes[:].bitcast(FP8X4),
+                scales=scales[:],
+                in_=grouped[q][:].rearrange("p t j -> p (t j)"),
+            )
+            xk_mx[q] = (codes, scales)
+
+        def multiply(n):
+            chunk, i = divmod(n, CHUNK_TILES)
+            tokens = slice(i * P, (i + 1) * P)
+            accs[n] = []
+            for half in range(N_TILES):
+                cols = slice(half * N_TILE, (half + 1) * N_TILE)
+                acc = products.tile([P, N_TILE], F32, tag="acc")
+                for g in range(PASSES):
+                    codes, scales = xk_mx[chunk * PASSES + g]
+                    nc.tensor.matmul_mx(
+                        out=acc[:],
+                        lhsT=codes[:, tokens].bitcast(FP8X4),
+                        lhsT_scale=scales[:, tokens],
+                        rhs=w_codes[:, g, cols].bitcast(FP8X4),
+                        rhs_scale=w_scales[:, g, cols],
+                        start=(g == 0),
+                        stop=(g == PASSES - 1),
+                    )
+                accs[n].append(acc)
+
+        def times_k_k(n):
+            pair, t = divmod(n, PAIR)
+            if t == 0:
+                scaled[pair] = results.tile([P, PAIR, C], F32, name="scaled")
+            for half in range(N_TILES):
+                cols = slice(half * N_TILE, (half + 1) * N_TILE)
+                nc.vector.tensor_tensor(
+                    out=scaled[pair][:, t, cols], in0=accs[n][half][:], in1=k_k_sb[:, cols], op=ALU.mult
+                )
+
+        def sum_squares(n):
+            pair, t = divmod(n, PAIR)
+            if t == 0:
+                square_sums[pair] = norms.tile([P, PAIR * HEADS], F32, name="square_sums")
+            squares = scratch.tile([P, C], BF16)
+            for h in range(HEADS):
+                head = slice(h * HEAD, (h + 1) * HEAD)
+                nc.scalar.activation(
+                    out=squares[:, head],
+                    in_=scaled[pair][:, t, head],
+                    func=ACT.Square,
+                    accum_out=square_sums[pair][:, t * HEADS + h : t * HEADS + h + 1],
+                )
+
+        def invert_norms(pair):
+            inverse[pair] = norms.tile([P, PAIR * HEADS], F32, name="inverse")
+            nc.scalar.activation(
+                out=inverse[pair][:],
+                in_=square_sums[pair][:],
+                func=ACT.Abs_reciprocal_sqrt,
+                bias=TINY,
+            )
+
+        def normalise_and_store(pair, engine):
+            s, first_tile = divmod(pair * PAIR, T // P)
+            engine.tensor_scalar_min(
+                out=inverse[pair][:], in0=inverse[pair][:], scalar1=1.0 / NORM_FLOOR
+            )
+            by_head = scaled[pair][:].rearrange("p t (h d) -> p (t h) d", d=HEAD)
+            for t in range(PAIR):
+                for piece in range(t * HEADS // PIECE_HEADS, (t + 1) * HEADS // PIECE_HEADS):
+                    heads = slice(piece * PIECE_HEADS, (piece + 1) * PIECE_HEADS)
+                    engine.tensor_tensor(
+                        out=by_head[:, heads, :],
+                        in0=by_head[:, heads, :],
+                        in1=inverse[pair][:, heads].unsqueeze(2).to_broadcast([P, PIECE_HEADS, HEAD]),
+                        op=ALU.mult,
+                    )
+                nc.sync.dma_start(out=out_view[:, s, first_tile + t, :], in_=scaled[pair][:, t, :])
+
+        def due(index, count):
+            return 0 <= index < count
+
+        for tick in range(TICKS):
+            if due(tick, STEPS):
+                flip(tick)
+            for b in (2 * (tick - 1), 2 * (tick - 1) + 1):
+                if due(b, PASSES * W_QUARTERS):
+                    flip_weights(b)
+            if due(tick - MULTIPLY_LAG, STEPS):
+                multiply(tick - MULTIPLY_LAG)
+
+            if due(tick - SHIFT_LAG, STEPS):
+                shift(tick - SHIFT_LAG)
+            for b in (2 * (tick - 2), 2 * (tick - 2) + 1):
+                if due(b, PASSES * W_QUARTERS):
+                    group_weights(b)
+
+            m = tick - BLEND_LAG
+            if due(m, STEPS):
+                blend(m)
+            q = tick - QUANT_LAG
+            if due(q, STEPS) and q % PAIRED == PAIRED - 1:
+                quantise(q // PAIRED)
+            if tick in (4, 6):
+                quantise_weights((tick - 4) // 2)
+            if due(tick - K_K_LAG, STEPS):
+                times_k_k(tick - K_K_LAG)
+            if due(m, STEPS) and m % PAIRED == PAIRED - 1:
+                regroup(m // PAIRED)
+
+            if due(tick - SUMS_LAG, STEPS):
+                sum_squares(tick - SUMS_LAG)
+                if (tick - SUMS_LAG) % PAIR == PAIR - 1:
+                    invert_norms((tick - SUMS_LAG) // PAIR)
+
+            n = tick - NORMALISE_LAG
+            if due(n, STEPS) and n % PAIR == PAIR - 1:
+                normalise_and_store(n // PAIR, nc.vector if n >= STEPS - 8 else nc.gpsimd)

@@ -272,21 +272,42 @@ def tile_full_tmix_params_pa_t_kernel(tc, x, x_k, Wk, k_k, out):
                 bias=TINY,
             )
 
-        def normalise_and_store(pair, engine):
-            s, first_tile = divmod(pair * PAIR, T // P)
-            engine.tensor_scalar_min(
+        def clamp_inverse(pair):
+            nc.vector.tensor_scalar_min(
                 out=inverse[pair][:], in0=inverse[pair][:], scalar1=1.0 / NORM_FLOOR
             )
-            by_head = scaled[pair][:].rearrange("p t (h d) -> p (t h) d", d=HEAD)
+
+        def shares(pair):
+            gpsimd, scalar = (16, 0) if pair >= STEPS // PAIR - 4 else (24, 4)
+            return (0, gpsimd), (gpsimd, gpsimd + scalar), (gpsimd + scalar, PAIR * HEADS)
+
+        def by_head(pair):
+            return scaled[pair][:].rearrange("p t (h d) -> p (t h) d", d=HEAD)
+
+        def normalise(pair, engine, low, high):
+            for start in range(low, high, PIECE_HEADS):
+                heads = slice(start, min(start + PIECE_HEADS, high))
+                engine.tensor_tensor(
+                    out=by_head(pair)[:, heads, :],
+                    in0=by_head(pair)[:, heads, :],
+                    in1=inverse[pair][:, heads]
+                    .unsqueeze(2)
+                    .to_broadcast([P, heads.stop - heads.start, HEAD]),
+                    op=ALU.mult,
+                )
+
+        def normalise_on_scalar(pair, low, high):
+            for h in range(low, high):
+                nc.scalar.activation(
+                    out=by_head(pair)[:, h, :],
+                    in_=by_head(pair)[:, h, :],
+                    func=ACT.Copy,
+                    scale=inverse[pair][:, h : h + 1],
+                )
+
+        def store(pair):
+            s, first_tile = divmod(pair * PAIR, T // P)
             for t in range(PAIR):
-                for piece in range(t * HEADS // PIECE_HEADS, (t + 1) * HEADS // PIECE_HEADS):
-                    heads = slice(piece * PIECE_HEADS, (piece + 1) * PIECE_HEADS)
-                    engine.tensor_tensor(
-                        out=by_head[:, heads, :],
-                        in0=by_head[:, heads, :],
-                        in1=inverse[pair][:, heads].unsqueeze(2).to_broadcast([P, PIECE_HEADS, HEAD]),
-                        op=ALU.mult,
-                    )
                 nc.sync.dma_start(out=out_view[:, s, first_tile + t, :], in_=scaled[pair][:, t, :])
 
         def due(index, count):
@@ -310,6 +331,12 @@ def tile_full_tmix_params_pa_t_kernel(tc, x, x_k, Wk, k_k, out):
             m = tick - BLEND_LAG
             if due(m, STEPS):
                 blend(m)
+            n = tick - NORMALISE_LAG
+            pair_due = due(n, STEPS) and n % PAIR == PAIR - 1
+            if pair_due:
+                clamp_inverse(n // PAIR)
+                on_gpsimd, on_scalar, on_vector = shares(n // PAIR)
+                normalise(n // PAIR, nc.gpsimd, *on_gpsimd)
             q = tick - QUANT_LAG
             if due(q, STEPS) and q % PAIRED == PAIRED - 1:
                 quantise(q // PAIRED)
@@ -325,6 +352,7 @@ def tile_full_tmix_params_pa_t_kernel(tc, x, x_k, Wk, k_k, out):
                 if (tick - SUMS_LAG) % PAIR == PAIR - 1:
                     invert_norms((tick - SUMS_LAG) // PAIR)
 
-            n = tick - NORMALISE_LAG
-            if due(n, STEPS) and n % PAIR == PAIR - 1:
-                normalise_and_store(n // PAIR, nc.vector if n >= STEPS - 8 else nc.gpsimd)
+            if pair_due:
+                normalise_on_scalar(n // PAIR, *on_scalar)
+                normalise(n // PAIR, nc.vector, *on_vector)
+                store(n // PAIR)

@@ -32,6 +32,7 @@ N_TILE = 512
 N_TILES = C // N_TILE
 PAIR = 2
 PIECE_HEADS = 8
+TENSOR_SEQS = (1, 2, 3)
 RUN = 4
 NORM_FLOOR = 1e-12
 TINY = 1e-34
@@ -39,10 +40,13 @@ TINY = 1e-34
 SHIFT_LAG = 1
 BLEND_LAG = 2
 QUANT_LAG = 3
+DIFFERENCE_LAG = 2
+ADD_LAG = 3
+TENSOR_QUANT_LAG = 5
 MULTIPLY_LAG = 7
 K_K_LAG = 8
 SUMS_LAG = 9
-NORMALISE_LAG = 10
+NORMALISE_LAG = 11
 TICKS = STEPS + NORMALISE_LAG + 1
 
 FLOPS = 2 * B * T * C * C
@@ -60,10 +64,11 @@ def tile_full_tmix_params_pa_t_kernel(tc, x, x_k, Wk, k_k, out):
         w_stage = ctx.enter_context(tc.tile_pool(name="w_stage", bufs=PASSES))
         mix_stage = ctx.enter_context(tc.tile_pool(name="mix_stage", bufs=2))
         quantised = ctx.enter_context(tc.tile_pool(name="quantised", bufs=3 * PASSES))
-        results = ctx.enter_context(tc.tile_pool(name="results", bufs=5))
+        results = ctx.enter_context(tc.tile_pool(name="results", bufs=6))
         norms = ctx.enter_context(tc.tile_pool(name="norms", bufs=4))
         scratch = ctx.enter_context(tc.tile_pool(name="scratch", bufs=2))
-        flipped = ctx.enter_context(tc.psum_pool(name="flipped", bufs=4))
+        flipped = ctx.enter_context(tc.psum_pool(name="flipped", bufs=2))
+        mixed = ctx.enter_context(tc.psum_pool(name="mixed", bufs=2))
         products = ctx.enter_context(tc.psum_pool(name="products", bufs=4))
 
         x_k_rows = keep.tile([P, K_PASS], BF16)
@@ -115,16 +120,33 @@ def tile_full_tmix_params_pa_t_kernel(tc, x, x_k, Wk, k_k, out):
         prev = keep.tile([P, PASSES, PAIRED, PAIRED, T + 8], F32)
         nc.vector.memset(prev[:, :, :, :, 0:8].rearrange("p g u e t -> p (g u e) t"), 0.0)
 
+        flat = keep.tile([P, T + 8, PACK], BF16)
+        nc.vector.memset(flat[:, 0:8, :], 0.0)
+
+        plus = keep.tile([P, PACK, P], BF16)
+        minus = keep.tile([P, PACK, P], BF16)
+        for sign, diagonal in ((1.0, plus), (-1.0, minus)):
+            for j in range(PACK):
+                nc.gpsimd.tensor_scalar(
+                    out=diagonal[:, j, :],
+                    in0=ident[:],
+                    scalar1=mix_prev[:, 0, j // PAIRED, j % PAIRED : j % PAIRED + 1],
+                    scalar2=sign,
+                    op0=ALU.mult,
+                    op1=ALU.mult,
+                )
+
         w_codes = keep.tile([P, PASSES, C], U32, align_bytes=64)
         w_scales = keep.tile([P, PASSES, C], U8, align_bytes=64)
 
         w_banks, w_grouped = {}, {}
+        differences = {}
         x_banks, planes, grouped, xk_mx = {}, {}, {}, {}
         accs, scaled, square_sums, inverse = {}, {}, {}, {}
 
         def flip_weights(b):
             g, quarter = divmod(b, W_QUARTERS)
-            w_banks[b] = flipped.tile([P, PAIRED, 2 * P], F32, tag="bank", name="w_bank")
+            w_banks[b] = products.tile([P, PAIRED, 2 * P], F32, tag="acc", name="w_bank")
             for u in range(PAIRED):
                 for r in range(W_QUARTER // P):
                     words = w_sb[:, quarter * (W_QUARTER // P) + r, :].bitcast(F32)
@@ -157,9 +179,23 @@ def tile_full_tmix_params_pa_t_kernel(tc, x, x_k, Wk, k_k, out):
             s, h = divmod(chunk, SEQ_CHUNKS)
             return chunk, g, u, s, h
 
+        def by_tensor(q):
+            chunk, g = divmod(q, PASSES)
+            return g == 0 and chunk // SEQ_CHUNKS in TENSOR_SEQS
+
         def flip(m):
             chunk, g, u, s, h = place(m)
             x_banks[m] = flipped.tile([P, PAIRED, 2 * P], F32, tag="bank", name="x_bank")
+            if by_tensor(m // PAIRED):
+                for i in range(PAIRED):
+                    words = x_sb[:, s, h * CHUNK_TILES + u * PAIRED + i, :].bitcast(F32)
+                    for v in range(PAIRED):
+                        nc.tensor.transpose(
+                            x_banks[m][:, v, i * P : (i + 1) * P],
+                            words[:, g * WORDS + v : (g + 1) * WORDS : PAIRED],
+                            ident[:],
+                        )
+                return
             bank = x_banks[m][:].rearrange("p u n -> p (u n)")
             for i in range(CHUNK_TILES):
                 words = x_sb[:, s, h * CHUNK_TILES + i, :].bitcast(F32)
@@ -175,6 +211,37 @@ def tile_full_tmix_params_pa_t_kernel(tc, x, x_k, Wk, k_k, out):
                 .rearrange("p u n -> p (u n)")
                 .bitcast(BF16)
                 .rearrange("p (t e) -> p e t", e=PAIRED)
+            )
+
+        def flatten(m):
+            chunk, g, u, s, h = place(m)
+            start = 1 + h * CHUNK + u * PAIRED * P
+            nc.scalar.copy(
+                out=flat[:, start : start + PAIRED * P, :].rearrange("p t j -> p (t j)").bitcast(F32),
+                in_=x_banks[m][:].rearrange("p v t -> p t v"),
+            )
+
+        def difference(q, i):
+            start = (q // PASSES % SEQ_CHUNKS) * CHUNK + i * P
+            acc = mixed.tile([P, PACK, P], F32, name="difference")
+            for j in range(PACK):
+                nc.tensor.matmul(
+                    acc[:, j, :], plus[:, j, :], flat[:, start : start + P, j], start=True, stop=False
+                )
+                nc.tensor.matmul(
+                    acc[:, j, :], minus[:, j, :], flat[:, start + 1 : start + 1 + P, j], start=False, stop=True
+                )
+            differences[q, i] = acc
+
+        def add_difference(q, i):
+            start = (q // PASSES % SEQ_CHUNKS) * CHUNK + i * P
+            if i == 0:
+                grouped[q] = mix_stage.tile([P, CHUNK, PACK], BF16, align_bytes=64, name="grouped")
+            nc.vector.tensor_tensor(
+                out=grouped[q][:, i * P : (i + 1) * P, :],
+                in0=differences[q, i][:].rearrange("p j t -> p t j"),
+                in1=flat[:, 1 + start : 1 + start + P, :],
+                op=ALU.add,
             )
 
         def shift(m):
@@ -313,39 +380,57 @@ def tile_full_tmix_params_pa_t_kernel(tc, x, x_k, Wk, k_k, out):
         def due(index, count):
             return 0 <= index < count
 
+        def halves(index):
+            q, second = divmod(index, PAIRED)
+            if due(index, STEPS) and by_tensor(q):
+                return [(q, (2, 3) if second else (0, 1))]
+            return []
+
         for tick in range(TICKS):
+            if due(tick - MULTIPLY_LAG, STEPS):
+                multiply(tick - MULTIPLY_LAG)
+            for q, tiles in halves(tick - DIFFERENCE_LAG):
+                for i in tiles:
+                    difference(q, i)
             if due(tick, STEPS):
                 flip(tick)
             for b in (2 * (tick - 1), 2 * (tick - 1) + 1):
                 if due(b, PASSES * W_QUARTERS):
                     flip_weights(b)
-            if due(tick - MULTIPLY_LAG, STEPS):
-                multiply(tick - MULTIPLY_LAG)
 
             if due(tick - SHIFT_LAG, STEPS):
-                shift(tick - SHIFT_LAG)
+                if by_tensor((tick - SHIFT_LAG) // PAIRED):
+                    flatten(tick - SHIFT_LAG)
+                else:
+                    shift(tick - SHIFT_LAG)
             for b in (2 * (tick - 2), 2 * (tick - 2) + 1):
                 if due(b, PASSES * W_QUARTERS):
                     group_weights(b)
 
             m = tick - BLEND_LAG
-            if due(m, STEPS):
+            if due(m, STEPS) and not by_tensor(m // PAIRED):
                 blend(m)
             n = tick - NORMALISE_LAG
             pair_due = due(n, STEPS) and n % PAIR == PAIR - 1
-            if pair_due:
-                clamp_inverse(n // PAIR)
-                on_gpsimd, on_scalar, on_vector = shares(n // PAIR)
-                normalise(n // PAIR, nc.gpsimd, *on_gpsimd)
             q = tick - QUANT_LAG
-            if due(q, STEPS) and q % PAIRED == PAIRED - 1:
+            if due(q, STEPS) and q % PAIRED == PAIRED - 1 and not by_tensor(q // PAIRED):
+                quantise(q // PAIRED)
+            q = tick - TENSOR_QUANT_LAG
+            if due(q, STEPS) and q % PAIRED == 0 and by_tensor(q // PAIRED):
                 quantise(q // PAIRED)
             if tick in (4, 6):
                 quantise_weights((tick - 4) // 2)
             if due(tick - K_K_LAG, STEPS):
                 times_k_k(tick - K_K_LAG)
-            if due(m, STEPS) and m % PAIRED == PAIRED - 1:
+            if pair_due:
+                clamp_inverse(n // PAIR)
+                on_gpsimd, on_scalar, on_vector = shares(n // PAIR)
+                normalise(n // PAIR, nc.gpsimd, *on_gpsimd)
+            if due(m, STEPS) and m % PAIRED == PAIRED - 1 and not by_tensor(m // PAIRED):
                 regroup(m // PAIRED)
+            for q, tiles in halves(tick - ADD_LAG):
+                for i in tiles:
+                    add_difference(q, i)
 
             if due(tick - SUMS_LAG, STEPS):
                 sum_squares(tick - SUMS_LAG)

@@ -29,9 +29,12 @@ STEPS = CHUNKS * BANKS
 W_QUARTER = 256
 W_QUARTERS = C // W_QUARTER
 N_TILE = 512
+VECTOR_HEADS = 12
+GPSIMD_HEADS = 14
 N_TILES = C // N_TILE
 PAIR = 2
-PIECE_HEADS = 8
+GROUP = CHUNK_TILES
+GROUPS = STEPS // GROUP
 TENSOR_SEQS = (1, 2, 3)
 RUN = 4
 NORM_FLOOR = 1e-12
@@ -39,15 +42,19 @@ TINY = 1e-34
 
 SHIFT_LAG = 1
 BLEND_LAG = 2
-QUANT_LAG = 3
-DIFFERENCE_LAG = 2
-ADD_LAG = 3
-TENSOR_QUANT_LAG = 5
-MULTIPLY_LAG = 7
-K_K_LAG = 8
-SUMS_LAG = 9
-NORMALISE_LAG = 11
-TICKS = STEPS + NORMALISE_LAG + 1
+W_LAG = 2
+W_RATE = 3
+DIFFERENCE_LAG = 1
+ADD_LAG = 2
+REGROUP_LAG = 5
+QUANT_LAG = 6
+MULTIPLY_LAG = 6
+K_K_LAG = 7
+SUMS_LAG = 8
+NORMALISE_LAG = 14
+GPSIMD_GROUPS = 5
+LAST_TICK = STEPS + 3
+TICKS = LAST_TICK + (GROUPS - GPSIMD_GROUPS) * GROUP // PAIR
 
 FLOPS = 2 * B * T * C * C
 
@@ -61,14 +68,12 @@ def tile_full_tmix_params_pa_t_kernel(tc, x, x_k, Wk, k_k, out):
     with ExitStack() as ctx:
         ctx.enter_context(tc.manual_schedule())
         keep = ctx.enter_context(tc.tile_pool(name="keep", bufs=1))
-        w_stage = ctx.enter_context(tc.tile_pool(name="w_stage", bufs=PASSES))
         mix_stage = ctx.enter_context(tc.tile_pool(name="mix_stage", bufs=2))
-        quantised = ctx.enter_context(tc.tile_pool(name="quantised", bufs=3 * PASSES))
-        results = ctx.enter_context(tc.tile_pool(name="results", bufs=6))
+        quantised = ctx.enter_context(tc.tile_pool(name="quantised", bufs=2))
+        results = ctx.enter_context(tc.tile_pool(name="results", bufs=12))
         norms = ctx.enter_context(tc.tile_pool(name="norms", bufs=4))
         scratch = ctx.enter_context(tc.tile_pool(name="scratch", bufs=2))
-        flipped = ctx.enter_context(tc.psum_pool(name="flipped", bufs=2))
-        mixed = ctx.enter_context(tc.psum_pool(name="mixed", bufs=2))
+        banks = ctx.enter_context(tc.psum_pool(name="banks", bufs=4))
         products = ctx.enter_context(tc.psum_pool(name="products", bufs=4))
 
         x_k_rows = keep.tile([P, K_PASS], BF16)
@@ -83,7 +88,7 @@ def tile_full_tmix_params_pa_t_kernel(tc, x, x_k, Wk, k_k, out):
             nc.sync.dma_start(out=x_sb[:, s, tiles, cols], in_=x_view[:, s, tiles, cols])
 
         first, second = slice(0, K_PASS), slice(K_PASS, C)
-        nc.sync.dma_start(out=x_k_rows[0:PASSES, :], in_=x_k.rearrange("(g c) -> g c", g=PASSES))
+        nc.scalar.dma_start(out=x_k_rows[0:PASSES, :], in_=x_k.rearrange("(g c) -> g c", g=PASSES))
         load_x(0, first)
         load_x(0, second)
         nc.sync.dma_start(out=w_sb[:, :, first], in_=w_view[:, :, first])
@@ -101,7 +106,7 @@ def tile_full_tmix_params_pa_t_kernel(tc, x, x_k, Wk, k_k, out):
         nc.scalar.activation(out=one[:], in_=one[:], func=ACT.Abs_reciprocal_sqrt)
 
         x_k_words = x_k_rows[:].bitcast(F32)
-        x_k_flipped = flipped.tile([P, PAIRED, 2 * P], F32, tag="bank")
+        x_k_flipped = banks.tile([P, PAIRED, 2 * P], F32, tag="bank")
         for u in range(PAIRED):
             nc.tensor.transpose(x_k_flipped[:, u, 0:P], x_k_words[:, u:WORDS:PAIRED], ident[:])
         mix_prev = keep.tile([P, PASSES, PAIRED, PAIRED], F32)
@@ -158,19 +163,23 @@ def tile_full_tmix_params_pa_t_kernel(tc, x, x_k, Wk, k_k, out):
 
         def group_weights(b):
             g, quarter = divmod(b, W_QUARTERS)
-            if quarter == 0:
-                w_grouped[g] = w_stage.tile([P, C, PACK], BF16, align_bytes=64, name="w_grouped")
-            rows = slice(quarter * W_QUARTER, (quarter + 1) * W_QUARTER)
+            half, second = divmod(quarter, 2)
+            if second == 0:
+                w_grouped[g, half] = results.tile(
+                    [P, N_TILE, PACK], BF16, align_bytes=64, tag="result", name="w_grouped"
+                )
+            rows = slice(second * W_QUARTER, (second + 1) * W_QUARTER)
             nc.scalar.copy(
-                out=w_grouped[g][:, rows, :].rearrange("p o j -> p (o j)").bitcast(F32),
+                out=w_grouped[g, half][:, rows, :].rearrange("p o j -> p (o j)").bitcast(F32),
                 in_=w_banks[b][:].rearrange("p u o -> p o u"),
             )
 
-        def quantise_weights(g):
+        def quantise_weights(g, half):
+            cols = slice(half * N_TILE, (half + 1) * N_TILE)
             nc.vector.quantize_mx(
-                out=w_codes[:, g, :].bitcast(FP8X4),
-                scales=w_scales[:, g, :],
-                in_=w_grouped[g][:].rearrange("p o j -> p (o j)"),
+                out=w_codes[:, g, cols].bitcast(FP8X4),
+                scales=w_scales[:, g, cols],
+                in_=w_grouped[g, half][:].rearrange("p o j -> p (o j)"),
             )
 
         def place(m):
@@ -185,7 +194,7 @@ def tile_full_tmix_params_pa_t_kernel(tc, x, x_k, Wk, k_k, out):
 
         def flip(m):
             chunk, g, u, s, h = place(m)
-            x_banks[m] = flipped.tile([P, PAIRED, 2 * P], F32, tag="bank", name="x_bank")
+            x_banks[m] = banks.tile([P, PAIRED, 2 * P], F32, tag="bank", name="x_bank")
             if by_tensor(m // PAIRED):
                 for i in range(PAIRED):
                     words = x_sb[:, s, h * CHUNK_TILES + u * PAIRED + i, :].bitcast(F32)
@@ -221,9 +230,12 @@ def tile_full_tmix_params_pa_t_kernel(tc, x, x_k, Wk, k_k, out):
                 in_=x_banks[m][:].rearrange("p v t -> p t v"),
             )
 
+        def new_grouped(chunk):
+            grouped[chunk] = mix_stage.tile([P, PASSES, CHUNK, PACK], BF16, align_bytes=64, name="grouped")
+
         def difference(q, i):
             start = (q // PASSES % SEQ_CHUNKS) * CHUNK + i * P
-            acc = mixed.tile([P, PACK, P], F32, name="difference")
+            acc = banks.tile([P, PACK, P], F32, tag="bank", name="difference")
             for j in range(PACK):
                 nc.tensor.matmul(
                     acc[:, j, :], plus[:, j, :], flat[:, start : start + P, j], start=True, stop=False
@@ -236,9 +248,9 @@ def tile_full_tmix_params_pa_t_kernel(tc, x, x_k, Wk, k_k, out):
         def add_difference(q, i):
             start = (q // PASSES % SEQ_CHUNKS) * CHUNK + i * P
             if i == 0:
-                grouped[q] = mix_stage.tile([P, CHUNK, PACK], BF16, align_bytes=64, name="grouped")
+                new_grouped(q // PASSES)
             nc.vector.tensor_tensor(
-                out=grouped[q][:, i * P : (i + 1) * P, :],
+                out=grouped[q // PASSES][:, q % PASSES, i * P : (i + 1) * P, :],
                 in0=differences[q, i][:].rearrange("p j t -> p t j"),
                 in1=flat[:, 1 + start : 1 + start + P, :],
                 op=ALU.add,
@@ -270,21 +282,23 @@ def tile_full_tmix_params_pa_t_kernel(tc, x, x_k, Wk, k_k, out):
                 )
 
         def regroup(q):
-            grouped[q] = mix_stage.tile([P, CHUNK, PACK], BF16, align_bytes=64, name="grouped")
+            chunk, g = divmod(q, PASSES)
+            if g == 0:
+                new_grouped(chunk)
             nc.vector.tensor_copy(
-                out=grouped[q][:].rearrange("p (c i) j -> p c j i", i=RUN),
+                out=grouped[chunk][:, g, :, :].rearrange("p (c i) j -> p c j i", i=RUN),
                 in_=planes[q][:].rearrange("p j (c i) -> p c j i", i=RUN),
             )
 
-        def quantise(q):
-            codes = quantised.tile([P, CHUNK], U32, align_bytes=64)
-            scales = quantised.tile([P, CHUNK], U8, align_bytes=64)
+        def quantise(chunk):
+            codes = quantised.tile([P, PASSES, CHUNK], U32, align_bytes=64)
+            scales = quantised.tile([P, PASSES, CHUNK], U8, align_bytes=64)
             nc.vector.quantize_mx(
-                out=codes[:].bitcast(FP8X4),
-                scales=scales[:],
-                in_=grouped[q][:].rearrange("p t j -> p (t j)"),
+                out=codes[:].rearrange("p g t -> p (g t)").bitcast(FP8X4),
+                scales=scales[:].rearrange("p g t -> p (g t)"),
+                in_=grouped[chunk][:].rearrange("p g t j -> p (g t j)"),
             )
-            xk_mx[q] = (codes, scales)
+            xk_mx[chunk] = (codes, scales)
 
         def multiply(n):
             chunk, i = divmod(n, CHUNK_TILES)
@@ -293,12 +307,12 @@ def tile_full_tmix_params_pa_t_kernel(tc, x, x_k, Wk, k_k, out):
             for half in range(N_TILES):
                 cols = slice(half * N_TILE, (half + 1) * N_TILE)
                 acc = products.tile([P, N_TILE], F32, tag="acc")
+                codes, scales = xk_mx[chunk]
                 for g in range(PASSES):
-                    codes, scales = xk_mx[chunk * PASSES + g]
                     nc.tensor.matmul_mx(
                         out=acc[:],
-                        lhsT=codes[:, tokens].bitcast(FP8X4),
-                        lhsT_scale=scales[:, tokens],
+                        lhsT=codes[:, g, tokens].bitcast(FP8X4),
+                        lhsT_scale=scales[:, g, tokens],
                         rhs=w_codes[:, g, cols].bitcast(FP8X4),
                         rhs_scale=w_scales[:, g, cols],
                         start=(g == 0),
@@ -306,76 +320,73 @@ def tile_full_tmix_params_pa_t_kernel(tc, x, x_k, Wk, k_k, out):
                     )
                 accs[n].append(acc)
 
-        def times_k_k(n):
-            pair, t = divmod(n, PAIR)
-            if t == 0:
-                scaled[pair] = results.tile([P, PAIR, C], F32, name="scaled")
-            for half in range(N_TILES):
-                cols = slice(half * N_TILE, (half + 1) * N_TILE)
-                nc.vector.tensor_tensor(
-                    out=scaled[pair][:, t, cols], in0=accs[n][half][:], in1=k_k_sb[:, cols], op=ALU.mult
-                )
+        def times_k_k(n, half):
+            if half == 0:
+                scaled[n] = results.tile([P, C], F32, align_bytes=64, tag="result", name="scaled")
+            cols = slice(half * N_TILE, (half + 1) * N_TILE)
+            nc.vector.tensor_tensor(
+                out=scaled[n][:, cols], in0=accs[n][half][:], in1=k_k_sb[:, cols], op=ALU.mult
+            )
 
         def sum_squares(n):
-            pair, t = divmod(n, PAIR)
+            group, t = divmod(n, GROUP)
             if t == 0:
-                square_sums[pair] = norms.tile([P, PAIR * HEADS], F32, name="square_sums")
+                square_sums[group] = norms.tile([P, GROUP * HEADS], F32, name="square_sums")
             squares = scratch.tile([P, C], BF16)
             for h in range(HEADS):
                 head = slice(h * HEAD, (h + 1) * HEAD)
                 nc.scalar.activation(
                     out=squares[:, head],
-                    in_=scaled[pair][:, t, head],
+                    in_=scaled[n][:, head],
                     func=ACT.Square,
-                    accum_out=square_sums[pair][:, t * HEADS + h : t * HEADS + h + 1],
+                    accum_out=square_sums[group][:, t * HEADS + h : t * HEADS + h + 1],
                 )
 
-        def invert_norms(pair):
-            inverse[pair] = norms.tile([P, PAIR * HEADS], F32, name="inverse")
+        def invert_norms(n):
+            group, t = divmod(n, GROUP)
+            if t == PAIR - 1:
+                inverse[group] = norms.tile([P, GROUP * HEADS], F32, name="inverse")
+            cols = slice((t + 1 - PAIR) * HEADS, (t + 1) * HEADS)
             nc.scalar.activation(
-                out=inverse[pair][:],
-                in_=square_sums[pair][:],
+                out=inverse[group][:, cols],
+                in_=square_sums[group][:, cols],
                 func=ACT.Abs_reciprocal_sqrt,
                 bias=TINY,
             )
 
-        def clamp_inverse(pair):
+        def clamp_inverse(n, count):
+            group, t = divmod(n, GROUP)
+            cols = slice(t * HEADS, (t + count) * HEADS)
             nc.vector.tensor_scalar_min(
-                out=inverse[pair][:], in0=inverse[pair][:], scalar1=1.0 / NORM_FLOOR
+                out=inverse[group][:, cols], in0=inverse[group][:, cols], scalar1=1.0 / NORM_FLOOR
             )
 
-        def shares(pair):
-            gpsimd, scalar = (16, 0) if pair >= STEPS // PAIR - 4 else (24, 4)
-            return (0, gpsimd), (gpsimd, gpsimd + scalar), (gpsimd + scalar, PAIR * HEADS)
+        def normalise(n, engine, low, high):
+            group, t = divmod(n, GROUP)
+            by_head = scaled[n][:].rearrange("p (h d) -> p h d", d=HEAD)[:, low:high, :]
+            engine.tensor_tensor(
+                out=by_head,
+                in0=by_head,
+                in1=inverse[group][:, t * HEADS + low : t * HEADS + high]
+                .unsqueeze(2)
+                .to_broadcast([P, high - low, HEAD]),
+                op=ALU.mult,
+            )
 
-        def by_head(pair):
-            return scaled[pair][:].rearrange("p t (h d) -> p (t h) d", d=HEAD)
-
-        def normalise(pair, engine, low, high):
-            for start in range(low, high, PIECE_HEADS):
-                heads = slice(start, min(start + PIECE_HEADS, high))
-                engine.tensor_tensor(
-                    out=by_head(pair)[:, heads, :],
-                    in0=by_head(pair)[:, heads, :],
-                    in1=inverse[pair][:, heads]
-                    .unsqueeze(2)
-                    .to_broadcast([P, heads.stop - heads.start, HEAD]),
-                    op=ALU.mult,
-                )
-
-        def normalise_on_scalar(pair, low, high):
+        def normalise_on_scalar(n, low, high):
+            group, t = divmod(n, GROUP)
             for h in range(low, high):
+                head = slice(h * HEAD, (h + 1) * HEAD)
                 nc.scalar.activation(
-                    out=by_head(pair)[:, h, :],
-                    in_=by_head(pair)[:, h, :],
+                    out=scaled[n][:, head],
+                    in_=scaled[n][:, head],
                     func=ACT.Copy,
-                    scale=inverse[pair][:, h : h + 1],
+                    scale=inverse[group][:, t * HEADS + h : t * HEADS + h + 1],
                 )
 
-        def store(pair):
-            s, first_tile = divmod(pair * PAIR, T // P)
-            for t in range(PAIR):
-                nc.sync.dma_start(out=out_view[:, s, first_tile + t, :], in_=scaled[pair][:, t, :])
+        def store(n):
+            s, i = divmod(n, T // P)
+            nc.sync.dma_start(out=out_view[:, s, i, :], in_=scaled[n][:])
 
         def due(index, count):
             return 0 <= index < count
@@ -386,58 +397,72 @@ def tile_full_tmix_params_pa_t_kernel(tc, x, x_k, Wk, k_k, out):
                 return [(q, (2, 3) if second else (0, 1))]
             return []
 
+        def w_due(index):
+            return range(max(0, W_RATE * index), min(W_RATE * (index + 1), PASSES * W_QUARTERS))
+
         for tick in range(TICKS):
-            if due(tick - MULTIPLY_LAG, STEPS):
-                multiply(tick - MULTIPLY_LAG)
-            for q, tiles in halves(tick - DIFFERENCE_LAG):
-                for i in tiles:
-                    difference(q, i)
-            if due(tick, STEPS):
-                flip(tick)
-            for b in (2 * (tick - 1), 2 * (tick - 1) + 1):
-                if due(b, PASSES * W_QUARTERS):
-                    flip_weights(b)
+            chunk, last = divmod(tick - QUANT_LAG, BANKS)
+            if due(chunk, CHUNKS) and last == 0:
+                quantise(chunk)
+            group, last = divmod(tick - NORMALISE_LAG, GROUP)
+            if due(group, GPSIMD_GROUPS) and last == 0:
+                clamp_inverse(group * GROUP, GROUP)
+                for n in range(group * GROUP, (group + 1) * GROUP):
+                    normalise(n, nc.gpsimd, 0, GPSIMD_HEADS)
 
             if due(tick - SHIFT_LAG, STEPS):
                 if by_tensor((tick - SHIFT_LAG) // PAIRED):
                     flatten(tick - SHIFT_LAG)
                 else:
                     shift(tick - SHIFT_LAG)
-            for b in (2 * (tick - 2), 2 * (tick - 2) + 1):
-                if due(b, PASSES * W_QUARTERS):
-                    group_weights(b)
+            for b in w_due(tick - W_LAG - 1):
+                group_weights(b)
+
+            if due(tick, STEPS):
+                flip(tick)
+            if due(tick - MULTIPLY_LAG, STEPS):
+                multiply(tick - MULTIPLY_LAG)
+            for q, tiles in halves(tick - DIFFERENCE_LAG):
+                for i in tiles:
+                    difference(q, i)
+            for b in w_due(tick - W_LAG):
+                flip_weights(b)
 
             m = tick - BLEND_LAG
+            n = tick - K_K_LAG
             if due(m, STEPS) and not by_tensor(m // PAIRED):
                 blend(m)
-            n = tick - NORMALISE_LAG
-            pair_due = due(n, STEPS) and n % PAIR == PAIR - 1
-            q = tick - QUANT_LAG
-            if due(q, STEPS) and q % PAIRED == PAIRED - 1 and not by_tensor(q // PAIRED):
-                quantise(q // PAIRED)
-            q = tick - TENSOR_QUANT_LAG
-            if due(q, STEPS) and q % PAIRED == 0 and by_tensor(q // PAIRED):
-                quantise(q // PAIRED)
-            if tick in (4, 6):
-                quantise_weights((tick - 4) // 2)
-            if due(tick - K_K_LAG, STEPS):
-                times_k_k(tick - K_K_LAG)
-            if pair_due:
-                clamp_inverse(n // PAIR)
-                on_gpsimd, on_scalar, on_vector = shares(n // PAIR)
-                normalise(n // PAIR, nc.gpsimd, *on_gpsimd)
-            if due(m, STEPS) and m % PAIRED == PAIRED - 1 and not by_tensor(m // PAIRED):
-                regroup(m // PAIRED)
             for q, tiles in halves(tick - ADD_LAG):
                 for i in tiles:
                     add_difference(q, i)
+            if due(n, STEPS):
+                times_k_k(n, 0)
+            chunk, last = divmod(tick - REGROUP_LAG, BANKS)
+            if due(chunk, CHUNKS) and last == 0:
+                for g in range(PASSES):
+                    if not by_tensor(chunk * PASSES + g):
+                        regroup(chunk * PASSES + g)
+            if due(n, STEPS):
+                times_k_k(n, 1)
+            if tick in (4, 5):
+                for half in range(N_TILES):
+                    quantise_weights(tick - 4, half)
 
-            if due(tick - SUMS_LAG, STEPS):
-                sum_squares(tick - SUMS_LAG)
-                if (tick - SUMS_LAG) % PAIR == PAIR - 1:
-                    invert_norms((tick - SUMS_LAG) // PAIR)
+            n = tick - SUMS_LAG
+            if due(n, STEPS):
+                sum_squares(n)
+                if n % PAIR == PAIR - 1:
+                    invert_norms(n)
+            group, half = divmod(tick - NORMALISE_LAG, GROUP)
+            if due(group, GPSIMD_GROUPS) and half < 2:
+                for n in range(group * GROUP + half * PAIR, group * GROUP + (half + 1) * PAIR):
+                    normalise_on_scalar(n, GPSIMD_HEADS, HEADS)
+                    store(n)
 
-            if pair_due:
-                normalise_on_scalar(n // PAIR, *on_scalar)
-                normalise(n // PAIR, nc.vector, *on_vector)
-                store(n // PAIR)
+            pair = tick - LAST_TICK + GPSIMD_GROUPS * GROUP // PAIR
+            if GPSIMD_GROUPS * GROUP <= pair * PAIR < STEPS and tick >= LAST_TICK:
+                clamp_inverse(pair * PAIR, PAIR)
+                for n in range(pair * PAIR, (pair + 1) * PAIR):
+                    normalise(n, nc.vector, 0, VECTOR_HEADS)
+                    normalise_on_scalar(n, VECTOR_HEADS, HEADS)
+                    store(n)

@@ -29,12 +29,14 @@ STEPS = CHUNKS * BANKS
 W_QUARTER = 256
 W_QUARTERS = C // W_QUARTER
 N_TILE = 512
+FIRST_HEADS = 4
 VECTOR_HEADS = 12
 GPSIMD_HEADS = 14
 N_TILES = C // N_TILE
 PAIR = 2
 GROUP = CHUNK_TILES
 GROUPS = STEPS // GROUP
+GPSIMD_PASSES = (0, 2)
 TENSOR_SEQS = (1, 2, 3)
 RUN = 4
 NORM_FLOOR = 1e-12
@@ -52,9 +54,11 @@ MULTIPLY_LAG = 6
 K_K_LAG = 7
 SUMS_LAG = 8
 NORMALISE_LAG = 14
-GPSIMD_GROUPS = 5
+GPSIMD_TILES = 21
+CLAMPED_GROUPS = 6
+LAST_LAG = 10
 LAST_TICK = STEPS + 3
-TICKS = LAST_TICK + (GROUPS - GPSIMD_GROUPS) * GROUP // PAIR
+TICKS = STEPS + LAST_LAG
 
 FLOPS = 2 * B * T * C * C
 
@@ -77,7 +81,7 @@ def tile_full_tmix_params_pa_t_kernel(tc, x, x_k, Wk, k_k, out):
         products = ctx.enter_context(tc.psum_pool(name="products", bufs=4))
 
         x_k_rows = keep.tile([P, K_PASS], BF16)
-        nc.vector.memset(x_k_rows[:], 0.0)
+        nc.vector.memset(x_k_rows[:].bitcast(F32), 0.0)
         x_sb = keep.tile([P, B, T // P, C], BF16)
         w_sb = keep.tile([P, C // P, C], BF16)
         k_k_sb = keep.tile([P, C], BF16)
@@ -88,7 +92,7 @@ def tile_full_tmix_params_pa_t_kernel(tc, x, x_k, Wk, k_k, out):
             nc.sync.dma_start(out=x_sb[:, s, tiles, cols], in_=x_view[:, s, tiles, cols])
 
         first, second = slice(0, K_PASS), slice(K_PASS, C)
-        nc.scalar.dma_start(out=x_k_rows[0:PASSES, :], in_=x_k.rearrange("(g c) -> g c", g=PASSES))
+        nc.sync.dma_start(out=x_k_rows[0:PASSES, :], in_=x_k.rearrange("(g c) -> g c", g=PASSES))
         load_x(0, first)
         load_x(0, second)
         nc.sync.dma_start(out=w_sb[:, :, first], in_=w_view[:, :, first])
@@ -147,7 +151,7 @@ def tile_full_tmix_params_pa_t_kernel(tc, x, x_k, Wk, k_k, out):
         w_banks, w_grouped = {}, {}
         differences = {}
         x_banks, planes, grouped, xk_mx = {}, {}, {}, {}
-        accs, scaled, square_sums, inverse = {}, {}, {}, {}
+        accs, scaled, squares, square_sums, inverse = {}, {}, {}, {}, {}
 
         def flip_weights(b):
             g, quarter = divmod(b, W_QUARTERS)
@@ -285,10 +289,19 @@ def tile_full_tmix_params_pa_t_kernel(tc, x, x_k, Wk, k_k, out):
             chunk, g = divmod(q, PASSES)
             if g == 0:
                 new_grouped(chunk)
-            nc.vector.tensor_copy(
-                out=grouped[chunk][:, g, :, :].rearrange("p (c i) j -> p c j i", i=RUN),
-                in_=planes[q][:].rearrange("p j (c i) -> p c j i", i=RUN),
-            )
+            for start in range(0, CHUNK, CHUNK // 2):
+                tokens = slice(start, start + CHUNK // 2)
+                out = grouped[chunk][:, g, tokens, :].rearrange("p (c i) j -> p c j i", i=RUN)
+                in_ = planes[q][:, :, tokens].rearrange("p j (c i) -> p c j i", i=RUN)
+                if q in GPSIMD_PASSES:
+                    nc.gpsimd.tensor_scalar(
+                        out=out, in0=in_, scalar1=1.0, scalar2=0.0, op0=ALU.mult, op1=ALU.add
+                    )
+                elif start == 0:
+                    nc.vector.tensor_copy(
+                        out=grouped[chunk][:, g, :, :].rearrange("p (c i) j -> p c j i", i=RUN),
+                        in_=planes[q][:].rearrange("p j (c i) -> p c j i", i=RUN),
+                    )
 
         def quantise(chunk):
             codes = quantised.tile([P, PASSES, CHUNK], U32, align_bytes=64)
@@ -328,15 +341,16 @@ def tile_full_tmix_params_pa_t_kernel(tc, x, x_k, Wk, k_k, out):
                 out=scaled[n][:, cols], in0=accs[n][half][:], in1=k_k_sb[:, cols], op=ALU.mult
             )
 
-        def sum_squares(n):
+        def sum_squares(n, low, high):
             group, t = divmod(n, GROUP)
-            if t == 0:
-                square_sums[group] = norms.tile([P, GROUP * HEADS], F32, name="square_sums")
-            squares = scratch.tile([P, C], BF16)
-            for h in range(HEADS):
+            if low == 0:
+                squares[n] = scratch.tile([P, C], BF16, name="squares")
+                if t == 0:
+                    square_sums[group] = norms.tile([P, GROUP * HEADS], F32, name="square_sums")
+            for h in range(low, high):
                 head = slice(h * HEAD, (h + 1) * HEAD)
                 nc.scalar.activation(
-                    out=squares[:, head],
+                    out=squares[n][:, head],
                     in_=scaled[n][:, head],
                     func=ACT.Square,
                     accum_out=square_sums[group][:, t * HEADS + h : t * HEADS + h + 1],
@@ -344,9 +358,9 @@ def tile_full_tmix_params_pa_t_kernel(tc, x, x_k, Wk, k_k, out):
 
         def invert_norms(n):
             group, t = divmod(n, GROUP)
-            if t == PAIR - 1:
+            if t == 0:
                 inverse[group] = norms.tile([P, GROUP * HEADS], F32, name="inverse")
-            cols = slice((t + 1 - PAIR) * HEADS, (t + 1) * HEADS)
+            cols = slice(t * HEADS, (t + 1) * HEADS)
             nc.scalar.activation(
                 out=inverse[group][:, cols],
                 in_=square_sums[group][:, cols],
@@ -400,14 +414,21 @@ def tile_full_tmix_params_pa_t_kernel(tc, x, x_k, Wk, k_k, out):
         def w_due(index):
             return range(max(0, W_RATE * index), min(W_RATE * (index + 1), PASSES * W_QUARTERS))
 
+        def last_tiles(index):
+            return [
+                n
+                for n in range(GPSIMD_TILES, STEPS)
+                if index == max(n + LAST_LAG, LAST_TICK + (n - GPSIMD_TILES) // 2)
+            ]
+
         for tick in range(TICKS):
             chunk, last = divmod(tick - QUANT_LAG, BANKS)
             if due(chunk, CHUNKS) and last == 0:
                 quantise(chunk)
             group, last = divmod(tick - NORMALISE_LAG, GROUP)
-            if due(group, GPSIMD_GROUPS) and last == 0:
+            if due(group, CLAMPED_GROUPS) and last == 0:
                 clamp_inverse(group * GROUP, GROUP)
-                for n in range(group * GROUP, (group + 1) * GROUP):
+                for n in range(group * GROUP, min((group + 1) * GROUP, GPSIMD_TILES)):
                     normalise(n, nc.gpsimd, 0, GPSIMD_HEADS)
 
             if due(tick - SHIFT_LAG, STEPS):
@@ -428,6 +449,9 @@ def tile_full_tmix_params_pa_t_kernel(tc, x, x_k, Wk, k_k, out):
             for b in w_due(tick - W_LAG):
                 flip_weights(b)
 
+            for n in last_tiles(tick):
+                if n >= CLAMPED_GROUPS * GROUP:
+                    clamp_inverse(n, 1)
             m = tick - BLEND_LAG
             n = tick - K_K_LAG
             if due(m, STEPS) and not by_tensor(m // PAIRED):
@@ -435,34 +459,37 @@ def tile_full_tmix_params_pa_t_kernel(tc, x, x_k, Wk, k_k, out):
             for q, tiles in halves(tick - ADD_LAG):
                 for i in tiles:
                     add_difference(q, i)
+            if m % PAIRED == 1 and m // PAIRED in GPSIMD_PASSES:
+                regroup(m // PAIRED)
             if due(n, STEPS):
                 times_k_k(n, 0)
             chunk, last = divmod(tick - REGROUP_LAG, BANKS)
             if due(chunk, CHUNKS) and last == 0:
                 for g in range(PASSES):
-                    if not by_tensor(chunk * PASSES + g):
+                    if not by_tensor(chunk * PASSES + g) and chunk * PASSES + g not in GPSIMD_PASSES:
                         regroup(chunk * PASSES + g)
             if due(n, STEPS):
                 times_k_k(n, 1)
+            for n in last_tiles(tick):
+                normalise(n, nc.vector, 0, VECTOR_HEADS)
             if tick in (4, 5):
                 for half in range(N_TILES):
                     quantise_weights(tick - 4, half)
 
             n = tick - SUMS_LAG
             if due(n, STEPS):
-                sum_squares(n)
-                if n % PAIR == PAIR - 1:
-                    invert_norms(n)
+                sum_squares(n, 0, FIRST_HEADS)
+            if due(n - 1, STEPS):
+                invert_norms(n - 1)
+            if due(n, STEPS):
+                sum_squares(n, FIRST_HEADS, HEADS)
             group, half = divmod(tick - NORMALISE_LAG, GROUP)
-            if due(group, GPSIMD_GROUPS) and half < 2:
+            if due(group, CLAMPED_GROUPS) and half < 2:
                 for n in range(group * GROUP + half * PAIR, group * GROUP + (half + 1) * PAIR):
-                    normalise_on_scalar(n, GPSIMD_HEADS, HEADS)
-                    store(n)
+                    if n < GPSIMD_TILES:
+                        normalise_on_scalar(n, GPSIMD_HEADS, HEADS)
+                        store(n)
 
-            pair = tick - LAST_TICK + GPSIMD_GROUPS * GROUP // PAIR
-            if GPSIMD_GROUPS * GROUP <= pair * PAIR < STEPS and tick >= LAST_TICK:
-                clamp_inverse(pair * PAIR, PAIR)
-                for n in range(pair * PAIR, (pair + 1) * PAIR):
-                    normalise(n, nc.vector, 0, VECTOR_HEADS)
-                    normalise_on_scalar(n, VECTOR_HEADS, HEADS)
-                    store(n)
+            for n in last_tiles(tick):
+                normalise_on_scalar(n, VECTOR_HEADS, HEADS)
+                store(n)

from contextlib import ExitStack

import concourse.mybir as mybir
from concourse.masks import make_identity

FP8X4 = mybir.dt.float8_e4m3fn_x4
BF16 = mybir.dt.bfloat16
F32 = mybir.dt.float32
U32 = mybir.dt.uint32
U8 = mybir.dt.uint8
ALU = mybir.AluOpType
ACT = mybir.ActivationFunctionType

P = 128
B, T, C = 4, 1024, 1024
HEAD = 64
HEADS = C // HEAD
PACK = 4
PAIRED = 2
K_PASS = P * PACK
PASSES = C // K_PASS
WORDS = K_PASS // PAIRED
CHUNK = 512
CHUNKS = B * T // CHUNK
SEQ_CHUNKS = T // CHUNK
CHUNK_TILES = CHUNK // P
BANKS = PASSES * PAIRED
STEPS = CHUNKS * BANKS
W_QUARTER = 256
W_QUARTERS = C // W_QUARTER
N_TILE = 512
FIRST_HEADS = 4
VECTOR_HEADS = 12
GPSIMD_HEADS = 14
N_TILES = C // N_TILE
PAIR = 2
GROUP = CHUNK_TILES
GROUPS = STEPS // GROUP
GPSIMD_PASSES = (0, 2)
TENSOR_SEQS = (1, 2, 3)
RUN = 4
NORM_FLOOR = 1e-12
TINY = 1e-34

SHIFT_LAG = 1
BLEND_LAG = 2
W_LAG = 2
W_RATE = 3
DIFFERENCE_LAG = 1
ADD_LAG = 2
REGROUP_LAG = 5
QUANT_LAG = 6
MULTIPLY_LAG = 6
K_K_LAG = 7
SUMS_LAG = 8
NORMALISE_LAG = 14
GPSIMD_TILES = 21
CLAMPED_GROUPS = 6
LAST_LAG = 10
LAST_TICK = STEPS + 3
TICKS = STEPS + LAST_LAG

FLOPS = 2 * B * T * C * C


def tile_full_tmix_params_pa_t_kernel(tc, x, x_k, Wk, k_k, out):
    nc = tc.nc
    x_view = x.rearrange("b (i p) c -> p b i c", p=P)
    w_view = Wk.rearrange("(r p) c -> p r c", p=P)
    out_view = out.rearrange("b (i p) c -> p b i c", p=P)

    with ExitStack() as ctx:
        ctx.enter_context(tc.manual_schedule())
        keep = ctx.enter_context(tc.tile_pool(name="keep", bufs=1))
        mix_stage = ctx.enter_context(tc.tile_pool(name="mix_stage", bufs=2))
        quantised = ctx.enter_context(tc.tile_pool(name="quantised", bufs=2))
        results = ctx.enter_context(tc.tile_pool(name="results", bufs=12))
        norms = ctx.enter_context(tc.tile_pool(name="norms", bufs=4))
        scratch = ctx.enter_context(tc.tile_pool(name="scratch", bufs=2))
        banks = ctx.enter_context(tc.psum_pool(name="banks", bufs=4))
        products = ctx.enter_context(tc.psum_pool(name="products", bufs=4))

        x_k_rows = keep.tile([P, K_PASS], BF16)
        nc.vector.memset(x_k_rows[:].bitcast(F32), 0.0)
        x_sb = keep.tile([P, B, T // P, C], BF16)
        w_sb = keep.tile([P, C // P, C], BF16)
        k_k_sb = keep.tile([P, C], BF16)

        def load_x(chunk, cols):
            s, h = divmod(chunk, SEQ_CHUNKS)
            tiles = slice(h * CHUNK_TILES, (h + 1) * CHUNK_TILES)
            nc.sync.dma_start(out=x_sb[:, s, tiles, cols], in_=x_view[:, s, tiles, cols])

        first, second = slice(0, K_PASS), slice(K_PASS, C)
        nc.sync.dma_start(out=x_k_rows[0:PASSES, :], in_=x_k.rearrange("(g c) -> g c", g=PASSES))
        load_x(0, first)
        load_x(0, second)
        nc.sync.dma_start(out=w_sb[:, :, first], in_=w_view[:, :, first])
        nc.sync.dma_start(out=w_sb[:, :, second], in_=w_view[:, :, second])
        load_x(1, slice(0, C))
        nc.sync.dma_start(out=k_k_sb[:], in_=k_k.partition_broadcast(P))
        for chunk in range(2, CHUNKS):
            load_x(chunk, slice(0, C))

        ident = keep.tile([P, P], F32)
        make_identity(nc, ident[:])

        one = keep.tile([P, 1], F32)
        nc.vector.memset(one[:], 1.0)
        nc.scalar.activation(out=one[:], in_=one[:], func=ACT.Abs_reciprocal_sqrt)

        x_k_words = x_k_rows[:].bitcast(F32)
        x_k_flipped = banks.tile([P, PAIRED, 2 * P], F32, tag="bank")
        for u in range(PAIRED):
            nc.tensor.transpose(x_k_flipped[:, u, 0:P], x_k_words[:, u:WORDS:PAIRED], ident[:])
        mix_prev = keep.tile([P, PASSES, PAIRED, PAIRED], F32)
        mix_here = keep.tile([P, PASSES, PAIRED, PAIRED], F32)
        nc.vector.tensor_copy(
            out=mix_prev[:].rearrange("p g u e -> p u g e"),
            in_=x_k_flipped[:]
            .rearrange("p u n -> p (u n)")
            .bitcast(BF16)
            .rearrange("p (u n e) -> p u n e", u=PAIRED, e=PAIRED)[:, :, 0:PASSES, :],
        )
        nc.vector.tensor_scalar(
            out=mix_here[:], in0=mix_prev[:], scalar1=-1.0, scalar2=1.0, op0=ALU.mult, op1=ALU.add
        )

        prev = keep.tile([P, PASSES, PAIRED, PAIRED, T + 8], F32)
        nc.vector.memset(prev[:, :, :, :, 0:8].rearrange("p g u e t -> p (g u e) t"), 0.0)

        flat = keep.tile([P, T + 8, PACK], BF16)
        nc.vector.memset(flat[:, 0:8, :], 0.0)

        plus = keep.tile([P, PACK, P], BF16)
        minus = keep.tile([P, PACK, P], BF16)
        for sign, diagonal in ((1.0, plus), (-1.0, minus)):
            for j in range(PACK):
                nc.gpsimd.tensor_scalar(
                    out=diagonal[:, j, :],
                    in0=ident[:],
                    scalar1=mix_prev[:, 0, j // PAIRED, j % PAIRED : j % PAIRED + 1],
                    scalar2=sign,
                    op0=ALU.mult,
                    op1=ALU.mult,
                )

        w_codes = keep.tile([P, PASSES, C], U32, align_bytes=64)
        w_scales = keep.tile([P, PASSES, C], U8, align_bytes=64)

        w_banks, w_grouped = {}, {}
        differences = {}
        x_banks, planes, grouped, xk_mx = {}, {}, {}, {}
        accs, scaled, squares, square_sums, inverse = {}, {}, {}, {}, {}

        def flip_weights(b):
            g, quarter = divmod(b, W_QUARTERS)
            w_banks[b] = products.tile([P, PAIRED, 2 * P], F32, tag="acc", name="w_bank")
            for u in range(PAIRED):
                for r in range(W_QUARTER // P):
                    words = w_sb[:, quarter * (W_QUARTER // P) + r, :].bitcast(F32)
                    nc.tensor.transpose(
                        w_banks[b][:, u, r * P : (r + 1) * P],
                        words[:, g * WORDS + u : (g + 1) * WORDS : PAIRED],
                        ident[:],
                    )

        def group_weights(b):
            g, quarter = divmod(b, W_QUARTERS)
            half, second = divmod(quarter, 2)
            if second == 0:
                w_grouped[g, half] = results.tile(
                    [P, N_TILE, PACK], BF16, align_bytes=64, tag="result", name="w_grouped"
                )
            rows = slice(second * W_QUARTER, (second + 1) * W_QUARTER)
            nc.scalar.copy(
                out=w_grouped[g, half][:, rows, :].rearrange("p o j -> p (o j)").bitcast(F32),
                in_=w_banks[b][:].rearrange("p u o -> p o u"),
            )

        def quantise_weights(g, half):
            cols = slice(half * N_TILE, (half + 1) * N_TILE)
            nc.vector.quantize_mx(
                out=w_codes[:, g, cols].bitcast(FP8X4),
                scales=w_scales[:, g, cols],
                in_=w_grouped[g, half][:].rearrange("p o j -> p (o j)"),
            )

        def place(m):
            chunk, within = divmod(m, BANKS)
            g, u = divmod(within, PAIRED)
            s, h = divmod(chunk, SEQ_CHUNKS)
            return chunk, g, u, s, h

        def by_tensor(q):
            chunk, g = divmod(q, PASSES)
            return g == 0 and chunk // SEQ_CHUNKS in TENSOR_SEQS

        def flip(m):
            chunk, g, u, s, h = place(m)
            x_banks[m] = banks.tile([P, PAIRED, 2 * P], F32, tag="bank", name="x_bank")
            if by_tensor(m // PAIRED):
                for i in range(PAIRED):
                    words = x_sb[:, s, h * CHUNK_TILES + u * PAIRED + i, :].bitcast(F32)
                    for v in range(PAIRED):
                        nc.tensor.transpose(
                            x_banks[m][:, v, i * P : (i + 1) * P],
                            words[:, g * WORDS + v : (g + 1) * WORDS : PAIRED],
                            ident[:],
                        )
                return
            bank = x_banks[m][:].rearrange("p u n -> p (u n)")
            for i in range(CHUNK_TILES):
                words = x_sb[:, s, h * CHUNK_TILES + i, :].bitcast(F32)
                nc.tensor.transpose(
                    bank[:, i * P : (i + 1) * P],
                    words[:, g * WORDS + u : (g + 1) * WORDS : PAIRED],
                    ident[:],
                )

        def bank_view(m):
            return (
                x_banks[m][:]
                .rearrange("p u n -> p (u n)")
                .bitcast(BF16)
                .rearrange("p (t e) -> p e t", e=PAIRED)
            )

        def flatten(m):
            chunk, g, u, s, h = place(m)
            start = 1 + h * CHUNK + u * PAIRED * P
            nc.scalar.copy(
                out=flat[:, start : start + PAIRED * P, :].rearrange("p t j -> p (t j)").bitcast(F32),
                in_=x_banks[m][:].rearrange("p v t -> p t v"),
            )

        def new_grouped(chunk):
            grouped[chunk] = mix_stage.tile([P, PASSES, CHUNK, PACK], BF16, align_bytes=64, name="grouped")

        def difference(q, i):
            start = (q // PASSES % SEQ_CHUNKS) * CHUNK + i * P
            acc = banks.tile([P, PACK, P], F32, tag="bank", name="difference")
            for j in range(PACK):
                nc.tensor.matmul(
                    acc[:, j, :], plus[:, j, :], flat[:, start : start + P, j], start=True, stop=False
                )
                nc.tensor.matmul(
                    acc[:, j, :], minus[:, j, :], flat[:, start + 1 : start + 1 + P, j], start=False, stop=True
                )
            differences[q, i] = acc

        def add_difference(q, i):
            start = (q // PASSES % SEQ_CHUNKS) * CHUNK + i * P
            if i == 0:
                new_grouped(q // PASSES)
            nc.vector.tensor_tensor(
                out=grouped[q // PASSES][:, q % PASSES, i * P : (i + 1) * P, :],
                in0=differences[q, i][:].rearrange("p j t -> p t j"),
                in1=flat[:, 1 + start : 1 + start + P, :],
                op=ALU.add,
            )

        def shift(m):
            chunk, g, u, s, h = place(m)
            for e in range(PAIRED):
                nc.scalar.activation(
                    out=prev[:, g, u, e, 1 + h * CHUNK : 1 + (h + 1) * CHUNK],
                    in_=bank_view(m)[:, e, :],
                    func=ACT.Copy,
                    scale=mix_prev[:, g, u, e : e + 1],
                )

        def blend(m):
            chunk, g, u, s, h = place(m)
            q = m // PAIRED
            if u == 0:
                planes[q] = mix_stage.tile([P, PACK, CHUNK], BF16, name="planes")
            for e in range(PAIRED):
                nc.vector.scalar_tensor_tensor(
                    out=planes[q][:, u * PAIRED + e, :],
                    in0=bank_view(m)[:, e, :],
                    scalar=mix_here[:, g, u, e : e + 1],
                    in1=prev[:, g, u, e, h * CHUNK : (h + 1) * CHUNK],
                    op0=ALU.mult,
                    op1=ALU.add,
                )

        def regroup(q):
            chunk, g = divmod(q, PASSES)
            if g == 0:
                new_grouped(chunk)
            for start in range(0, CHUNK, CHUNK // 2):
                tokens = slice(start, start + CHUNK // 2)
                out = grouped[chunk][:, g, tokens, :].rearrange("p (c i) j -> p c j i", i=RUN)
                in_ = planes[q][:, :, tokens].rearrange("p j (c i) -> p c j i", i=RUN)
                if q in GPSIMD_PASSES:
                    nc.gpsimd.tensor_scalar(
                        out=out, in0=in_, scalar1=1.0, scalar2=0.0, op0=ALU.mult, op1=ALU.add
                    )
                elif start == 0:
                    nc.vector.tensor_copy(
                        out=grouped[chunk][:, g, :, :].rearrange("p (c i) j -> p c j i", i=RUN),
                        in_=planes[q][:].rearrange("p j (c i) -> p c j i", i=RUN),
                    )

        def quantise(chunk):
            codes = quantised.tile([P, PASSES, CHUNK], U32, align_bytes=64)
            scales = quantised.tile([P, PASSES, CHUNK], U8, align_bytes=64)
            nc.vector.quantize_mx(
                out=codes[:].rearrange("p g t -> p (g t)").bitcast(FP8X4),
                scales=scales[:].rearrange("p g t -> p (g t)"),
                in_=grouped[chunk][:].rearrange("p g t j -> p (g t j)"),
            )
            xk_mx[chunk] = (codes, scales)

        def multiply(n):
            chunk, i = divmod(n, CHUNK_TILES)
            tokens = slice(i * P, (i + 1) * P)
            accs[n] = []
            for half in range(N_TILES):
                cols = slice(half * N_TILE, (half + 1) * N_TILE)
                acc = products.tile([P, N_TILE], F32, tag="acc")
                codes, scales = xk_mx[chunk]
                for g in range(PASSES):
                    nc.tensor.matmul_mx(
                        out=acc[:],
                        lhsT=codes[:, g, tokens].bitcast(FP8X4),
                        lhsT_scale=scales[:, g, tokens],
                        rhs=w_codes[:, g, cols].bitcast(FP8X4),
                        rhs_scale=w_scales[:, g, cols],
                        start=(g == 0),
                        stop=(g == PASSES - 1),
                    )
                accs[n].append(acc)

        def times_k_k(n, half):
            if half == 0:
                scaled[n] = results.tile([P, C], F32, align_bytes=64, tag="result", name="scaled")
            cols = slice(half * N_TILE, (half + 1) * N_TILE)
            nc.vector.tensor_tensor(
                out=scaled[n][:, cols], in0=accs[n][half][:], in1=k_k_sb[:, cols], op=ALU.mult
            )

        def sum_squares(n, low, high):
            group, t = divmod(n, GROUP)
            if low == 0:
                squares[n] = scratch.tile([P, C], BF16, name="squares")
                if t == 0:
                    square_sums[group] = norms.tile([P, GROUP * HEADS], F32, name="square_sums")
            for h in range(low, high):
                head = slice(h * HEAD, (h + 1) * HEAD)
                nc.scalar.activation(
                    out=squares[n][:, head],
                    in_=scaled[n][:, head],
                    func=ACT.Square,
                    accum_out=square_sums[group][:, t * HEADS + h : t * HEADS + h + 1],
                )

        def invert_norms(n):
            group, t = divmod(n, GROUP)
            if t == 0:
                inverse[group] = norms.tile([P, GROUP * HEADS], F32, name="inverse")
            cols = slice(t * HEADS, (t + 1) * HEADS)
            nc.scalar.activation(
                out=inverse[group][:, cols],
                in_=square_sums[group][:, cols],
                func=ACT.Abs_reciprocal_sqrt,
                bias=TINY,
            )

        def clamp_inverse(n, count):
            group, t = divmod(n, GROUP)
            cols = slice(t * HEADS, (t + count) * HEADS)
            nc.vector.tensor_scalar_min(
                out=inverse[group][:, cols], in0=inverse[group][:, cols], scalar1=1.0 / NORM_FLOOR
            )

        def normalise(n, engine, low, high):
            group, t = divmod(n, GROUP)
            by_head = scaled[n][:].rearrange("p (h d) -> p h d", d=HEAD)[:, low:high, :]
            engine.tensor_tensor(
                out=by_head,
                in0=by_head,
                in1=inverse[group][:, t * HEADS + low : t * HEADS + high]
                .unsqueeze(2)
                .to_broadcast([P, high - low, HEAD]),
                op=ALU.mult,
            )

        def normalise_on_scalar(n, low, high):
            group, t = divmod(n, GROUP)
            for h in range(low, high):
                head = slice(h * HEAD, (h + 1) * HEAD)
                nc.scalar.activation(
                    out=scaled[n][:, head],
                    in_=scaled[n][:, head],
                    func=ACT.Copy,
                    scale=inverse[group][:, t * HEADS + h : t * HEADS + h + 1],
                )

        def store(n):
            s, i = divmod(n, T // P)
            nc.sync.dma_start(out=out_view[:, s, i, :], in_=scaled[n][:])

        def due(index, count):
            return 0 <= index < count

        def halves(index):
            q, second = divmod(index, PAIRED)
            if due(index, STEPS) and by_tensor(q):
                return [(q, (2, 3) if second else (0, 1))]
            return []

        def w_due(index):
            return range(max(0, W_RATE * index), min(W_RATE * (index + 1), PASSES * W_QUARTERS))

        def last_tiles(index):
            return [
                n
                for n in range(GPSIMD_TILES, STEPS)
                if index == max(n + LAST_LAG, LAST_TICK + (n - GPSIMD_TILES) // 2)
            ]

        for tick in range(TICKS):
            chunk, last = divmod(tick - QUANT_LAG, BANKS)
            if due(chunk, CHUNKS) and last == 0:
                quantise(chunk)
            group, last = divmod(tick - NORMALISE_LAG, GROUP)
            if due(group, CLAMPED_GROUPS) and last == 0:
                clamp_inverse(group * GROUP, GROUP)
                for n in range(group * GROUP, min((group + 1) * GROUP, GPSIMD_TILES)):
                    normalise(n, nc.gpsimd, 0, GPSIMD_HEADS)

            if due(tick - SHIFT_LAG, STEPS):
                if by_tensor((tick - SHIFT_LAG) // PAIRED):
                    flatten(tick - SHIFT_LAG)
                else:
                    shift(tick - SHIFT_LAG)
            for b in w_due(tick - W_LAG - 1):
                group_weights(b)

            if due(tick, STEPS):
                flip(tick)
            if due(tick - MULTIPLY_LAG, STEPS):
                multiply(tick - MULTIPLY_LAG)
            for q, tiles in halves(tick - DIFFERENCE_LAG):
                for i in tiles:
                    difference(q, i)
            for b in w_due(tick - W_LAG):
                flip_weights(b)

            for n in last_tiles(tick):
                if n >= CLAMPED_GROUPS * GROUP:
                    clamp_inverse(n, 1)
            m = tick - BLEND_LAG
            n = tick - K_K_LAG
            if due(m, STEPS) and not by_tensor(m // PAIRED):
                blend(m)
            for q, tiles in halves(tick - ADD_LAG):
                for i in tiles:
                    add_difference(q, i)
            if m % PAIRED == 1 and m // PAIRED in GPSIMD_PASSES:
                regroup(m // PAIRED)
            if due(n, STEPS):
                times_k_k(n, 0)
            chunk, last = divmod(tick - REGROUP_LAG, BANKS)
            if due(chunk, CHUNKS) and last == 0:
                for g in range(PASSES):
                    if not by_tensor(chunk * PASSES + g) and chunk * PASSES + g not in GPSIMD_PASSES:
                        regroup(chunk * PASSES + g)
            if due(n, STEPS):
                times_k_k(n, 1)
            for n in last_tiles(tick):
                normalise(n, nc.vector, 0, VECTOR_HEADS)
            if tick in (4, 5):
                for half in range(N_TILES):
                    quantise_weights(tick - 4, half)

            n = tick - SUMS_LAG
            if due(n, STEPS):
                sum_squares(n, 0, FIRST_HEADS)
            if due(n - 1, STEPS):
                invert_norms(n - 1)
            if due(n, STEPS):
                sum_squares(n, FIRST_HEADS, HEADS)
            group, half = divmod(tick - NORMALISE_LAG, GROUP)
            if due(group, CLAMPED_GROUPS) and half < 2:
                for n in range(group * GROUP + half * PAIR, group * GROUP + (half + 1) * PAIR):
                    if n < GPSIMD_TILES:
                        normalise_on_scalar(n, GPSIMD_HEADS, HEADS)
                        store(n)

            for n in last_tiles(tick):
                normalise_on_scalar(n, VECTOR_HEADS, HEADS)
                store(n)
